import numpy as np
import ml_dtypes


def mxq(x, axis, fmt="e4m3"):
    dtype, down = {"e4m3": (ml_dtypes.float8_e4m3fn, 7), "e5m2": (ml_dtypes.float8_e5m2, 14)}[fmt]
    v = np.moveaxis(np.asarray(x, np.float32).astype(ml_dtypes.bfloat16).astype(np.float64), axis, -1)
    blocks = v.reshape(v.shape[:-1] + (-1, 32))
    amax = np.abs(blocks).max(-1, keepdims=True)
    byte = np.maximum(np.where(amax > 0, np.frexp(amax)[1] - 1 + 127, 0) - down, 1)
    scale = np.exp2(byte - 127.0)
    codes = (blocks / scale).astype(np.float32).astype(dtype).astype(np.float64)
    return np.moveaxis((codes * scale).reshape(v.shape), -1, axis)


WIDE = False


def mx_kscale(k):
    if not WIDE:
        return np.ones(k)
    levels = np.array([10, -10, 5, -5, 0])
    if k % 512:
        return np.exp2(np.random.permutation(np.resize(levels, k // 32))).repeat(32)
    a = np.empty((k // 512, 16))
    for p in range(k // 512):
        a[p, :8] = np.random.permutation(np.resize(levels, 8))
        for g in range(8):
            far = levels[np.abs(levels - a[p, g]) >= 10]
            a[p, g + 8] = far[np.random.randint(len(far))]
    return np.exp2(a.ravel()).repeat(32)


BF16 = ml_dtypes.bfloat16


def bf(x):
    return np.asarray(x, np.float32).astype(BF16)


def f64(x):
    return np.asarray(x).astype(np.float64)


B, S, HID, H, KV, D = 1, 512, 2048, 16, 4, 128
EPS = 1e-6
THETA = 10000.0
HALF = D // 2


def rotate_half(x):
    return np.concatenate([-x[..., HALF:], x[..., :HALF]], axis=-1)


def rms_norm(x, w=None):
    n = x * (1.0 / np.sqrt(np.mean(x * x, axis=-1, keepdims=True) + EPS))
    return n if w is None else n * w


def setup_inputs():
    s = mx_kscale(HID)
    c = 0.004 / np.sqrt(HID)
    inv_freq = 1.0 / THETA ** (np.arange(0, D, 2) / D)
    pos = np.random.randint(0, S) + np.arange(S)
    freqs = pos[:, None] * inv_freq[None, :]
    emb = np.concatenate([freqs, freqs], axis=-1)
    return {"hidden_states": bf(np.random.standard_normal((B, S, HID)) * s),
            "cos": bf(np.cos(emb)[None]),
            "sin": bf(np.sin(emb)[None]),
            "Wq": bf(np.random.standard_normal((H * D, HID)) * c / s[None, :]),
            "Wk": bf(np.random.standard_normal((KV * D, HID)) * c / s[None, :]),
            "Wv": bf(np.random.standard_normal((KV * D, HID)) * c / s[None, :]),
            "q_norm_w": bf(0.5 + 0.1 * np.random.standard_normal(D)),
            "k_norm_w": bf(0.5 + 0.1 * np.random.standard_normal(D))}


def reference(hidden_states, cos, sin, Wq, Wk, Wv, q_norm_w, k_norm_w):
    xq = mxq(f64(hidden_states), 2, "e4m3")
    cs = f64(cos)[:, :, None, :]
    sn = f64(sin)[:, :, None, :]
    q = (xq @ mxq(f64(Wq).T, 0, "e4m3")).reshape(B, S, H, D)
    k = (xq @ mxq(f64(Wk).T, 0, "e4m3")).reshape(B, S, KV, D)
    v = (xq @ mxq(f64(Wv).T, 0, "e4m3")).reshape(B, S, KV, D)
    q = rms_norm(q, f64(q_norm_w))
    q = q * cs + rotate_half(q) * sn
    k = rms_norm(k, f64(k_norm_w))
    k = k * cs + rotate_half(k) * sn
    v = rms_norm(v)
    return q.transpose(0, 2, 1, 3), k.transpose(0, 2, 1, 3), v.transpose(0, 2, 1, 3)

@@ -1,0 +1,299 @@
+from contextlib import ExitStack
+
+import concourse.mybir as mybir
+from concourse.masks import make_identity
+
+F32 = mybir.dt.float32
+BF16 = mybir.dt.bfloat16
+U32 = mybir.dt.uint32
+U8 = mybir.dt.uint8
+FP8X4 = mybir.dt.float8_e4m3fn_x4
+ACT = mybir.ActivationFunctionType
+ALU = mybir.AluOpType
+
+P = 128
+TOKENS = 512
+TOKEN_TILES = TOKENS // P
+HID = 2048
+D = 128
+HALF = D // 2
+EPS = 1e-6
+PASSES = HID // 512
+PASS_WORDS = 256
+UNIT_ROWS = 256
+UNIT_TILES = UNIT_ROWS // P
+X_UNITS = TOKENS // UNIT_ROWS
+Q_UNITS, K_UNITS, V_UNITS = 8, 2, 2
+W_UNITS = Q_UNITS + K_UNITS + V_UNITS
+UNITS = X_UNITS + W_UNITS
+LAG = 3
+LOADS_AHEAD = 6
+
+FLOPS = 2 * TOKENS * HID * (W_UNITS * UNIT_ROWS)
+
+
+def tile_refattention_pa_kernel(
+    tc, hidden_states, cos, sin, Wq, Wk, Wv, q_norm_w, k_norm_w, out_0, out_1, out_2
+):
+    nc = tc.nc
+    with ExitStack() as ctx:
+        const = ctx.enter_context(tc.tile_pool(name="const", bufs=1))
+        raw_pool = ctx.enter_context(tc.tile_pool(name="raw", bufs=1))
+        grouped_pool = ctx.enter_context(tc.tile_pool(name="grouped", bufs=4))
+        words_pool = ctx.enter_context(tc.tile_pool(name="words", bufs=4))
+        small = ctx.enter_context(tc.tile_pool(name="small", bufs=6))
+        squares_pool = ctx.enter_context(tc.tile_pool(name="squares", bufs=3))
+        terms_pool = ctx.enter_context(tc.tile_pool(name="terms", bufs=2))
+        stage_pool = ctx.enter_context(tc.tile_pool(name="stage", bufs=3))
+        flip_psum = ctx.enter_context(tc.psum_pool(name="flip", bufs=4))
+        acc_psum = ctx.enter_context(tc.psum_pool(name="acc", bufs=4))
+        ctx.enter_context(tc.manual_schedule())
+
+        gains_row = const.tile([P, 2 * D], BF16, name="gains_row")
+        nc.vector.memset(gains_row[:], 0.0)
+        nc.sync.dma_start(out=gains_row[0:1, 0:D], in_=q_norm_w.rearrange("(o d) -> o d", o=1))
+        nc.sync.dma_start(out=gains_row[0:1, D : 2 * D], in_=k_norm_w.rearrange("(o d) -> o d", o=1))
+        cos_sb = const.tile([P, TOKEN_TILES, D], BF16, name="cos_sb")
+        sin_sb = const.tile([P, TOKEN_TILES, D], BF16, name="sin_sb")
+        nc.sync.dma_start(
+            out=cos_sb[:], in_=cos.flatten_outer_dims().rearrange("(p t) d -> p t d", t=TOKEN_TILES)
+        )
+        nc.sync.dma_start(
+            out=sin_sb[:], in_=sin.flatten_outer_dims().rearrange("(p t) d -> p t d", t=TOKEN_TILES)
+        )
+
+        x_rows = hidden_states.flatten_outer_dims().rearrange("(p t) k -> p t k", t=TOKEN_TILES)
+        unit_rows = [x_rows[:, i * UNIT_TILES : (i + 1) * UNIT_TILES, :] for i in range(X_UNITS)]
+        for weight, units in ((Wq, Q_UNITS), (Wk, K_UNITS), (Wv, V_UNITS)):
+            for i in range(units):
+                rows = weight[i * UNIT_ROWS : (i + 1) * UNIT_ROWS, :]
+                unit_rows.append(rows.rearrange("(r p) k -> p r k", p=P))
+
+        raw = {}
+
+        def load(unit):
+            raw[unit] = raw_pool.tile([P, UNIT_TILES, HID], BF16, name="raw%d" % unit)
+            nc.sync.dma_start(out=raw[unit][:], in_=unit_rows[unit])
+
+        for unit in range(LOADS_AHEAD):
+            load(unit)
+
+        ident = const.tile([P, P], F32, name="ident")
+        make_identity(nc, ident[:])
+        ones = const.tile([P, P], BF16, name="ones")
+        nc.vector.memset(ones[:], 1.0)
+        eps_col = const.tile([P, 1], F32, name="eps_col")
+        nc.vector.memset(eps_col[:], EPS)
+        table_warm = const.tile([P, 1], F32, name="table_warm")
+        nc.scalar.activation(out=table_warm[:], in_=eps_col[:], func=ACT.Abs_reciprocal_sqrt)
+
+        gains_ps = flip_psum.tile([P, 2 * D], F32, tag="flip", name="gains_ps")
+        nc.tensor.matmul(out=gains_ps[:], lhsT=ones[:], rhs=gains_row[:], start=True, stop=True)
+        gains = const.tile([P, 2 * D], F32, name="gains")
+        minus_gains = const.tile([P, 2 * D], F32, name="minus_gains")
+        nc.scalar.copy(out=gains[:], in_=gains_ps[:])
+        nc.scalar.mul(out=minus_gains[:], in_=gains_ps[:], mul=-1.0)
+
+        rope = []
+        for which in range(2):
+            w_lo = slice(which * D, which * D + HALF)
+            w_hi = slice(which * D + HALF, (which + 1) * D)
+            table = const.tile([P, TOKEN_TILES, 2, D], F32, name="rope%d" % which)
+            for row, columns, angles, gain in (
+                (0, slice(0, HALF), cos_sb[:, :, 0:HALF], gains[:, w_lo]),
+                (0, slice(HALF, D), sin_sb[:, :, 0:HALF], minus_gains[:, w_hi]),
+                (1, slice(0, HALF), sin_sb[:, :, HALF:D], gains[:, w_lo]),
+                (1, slice(HALF, D), cos_sb[:, :, HALF:D], gains[:, w_hi]),
+            ):
+                nc.gpsimd.tensor_tensor(
+                    out=table[:, :, row, columns],
+                    in0=angles,
+                    in1=gain.unsqueeze(1).to_broadcast([P, TOKEN_TILES, HALF]),
+                    op=ALU.mult,
+                )
+            rope.append(table)
+
+        unit_out = []
+        for out, units in ((out_0, Q_UNITS), (out_1, K_UNITS), (out_2, V_UNITS)):
+            heads = out.rearrange("o h (p t) d -> p (o h) (t d)", t=TOKEN_TILES)
+            for i in range(units):
+                unit_out.append(heads[:, i * UNIT_TILES : (i + 1) * UNIT_TILES, :])
+
+        banks = {}
+        grouped = {}
+        codes = {}
+        scales = {}
+        accs = {}
+        sum_sq = {}
+        inv_rms = {}
+        terms = {}
+        stages = {}
+
+        def transposes(unit):
+            words = raw[unit][:].bitcast(F32)
+            for g in range(PASSES):
+                bank = flip_psum.tile([P, 2, UNIT_ROWS], F32, tag="flip", name="bank")
+                for r in range(UNIT_TILES):
+                    for u in range(2):
+                        every_second = slice(g * PASS_WORDS + u, (g + 1) * PASS_WORDS, 2)
+                        nc.tensor.transpose(
+                            bank[:, u, r * P : (r + 1) * P], words[:, r, every_second], ident[:]
+                        )
+                banks[(unit, g)] = bank
+
+        def copy_out(unit, g):
+            pair, i = divmod(g, 2)
+            if i == 0:
+                grouped[(unit, pair)] = grouped_pool.tile(
+                    [P, 2 * 4 * UNIT_ROWS], BF16, align_bytes=64, name="grouped"
+                )
+            grouped_words = grouped[(unit, pair)][:].bitcast(F32)
+            engine_copy = nc.vector.tensor_copy if (unit <= LAG and i == 1) else nc.scalar.copy
+            engine_copy(
+                out=grouped_words[:, i * 2 * UNIT_ROWS : (i + 1) * 2 * UNIT_ROWS].rearrange(
+                    "p (c u) -> p c u", u=2
+                ),
+                in_=banks[(unit, g)][:].rearrange("p u c -> p c u"),
+            )
+
+        def quantise(unit, pair):
+            if pair == 0:
+                pool = const if unit < X_UNITS else words_pool
+                codes[unit] = pool.tile(
+                    [P, PASSES * UNIT_ROWS], U32, align_bytes=64, name="codes%d" % min(unit, X_UNITS)
+                )
+                scales[unit] = pool.tile(
+                    [P, PASSES * UNIT_ROWS], U8, align_bytes=64, name="scales%d" % min(unit, X_UNITS)
+                )
+            columns = slice(pair * 2 * UNIT_ROWS, (pair + 1) * 2 * UNIT_ROWS)
+            nc.vector.quantize_mx(
+                out=codes[unit][:, columns].bitcast(FP8X4),
+                scales=scales[unit][:, columns],
+                in_=grouped[(unit, pair)][:],
+            )
+
+        def matmuls(m):
+            w = m + X_UNITS
+            for x_unit in range(X_UNITS):
+                acc = acc_psum.tile([P, UNIT_TILES, UNIT_ROWS], F32, tag="acc", name="acc")
+                for i in range(UNIT_TILES):
+                    for g in range(PASSES):
+                        tokens = slice(g * UNIT_ROWS + i * P, g * UNIT_ROWS + (i + 1) * P)
+                        features = slice(g * UNIT_ROWS, (g + 1) * UNIT_ROWS)
+                        nc.tensor.matmul_mx(
+                            out=acc[:, i, :],
+                            lhsT=codes[x_unit][:, tokens].bitcast(FP8X4),
+                            lhsT_scale=scales[x_unit][:, tokens],
+                            rhs=codes[w][:, features].bitcast(FP8X4),
+                            rhs_scale=scales[w][:, features],
+                            start=(g == 0),
+                            stop=(g == PASSES - 1),
+                        )
+                accs[(m, x_unit)] = acc
+
+        def sum_squares(m, x_unit):
+            acc = accs[(m, x_unit)]
+            sum_sq[(m, x_unit)] = small.tile([P, UNIT_TILES * UNIT_TILES], F32, name="sum_sq")
+            squares = squares_pool.tile([P, UNIT_TILES, UNIT_ROWS], F32, name="squares")
+            for i in range(UNIT_TILES):
+                for h in range(UNIT_TILES):
+                    column = i * UNIT_TILES + h
+                    nc.scalar.activation(
+                        out=squares[:, i, h * D : (h + 1) * D],
+                        in_=acc[:, i, h * D : (h + 1) * D],
+                        func=ACT.Square,
+                        accum_out=sum_sq[(m, x_unit)][:, column : column + 1],
+                    )
+
+        def inverse_rms(m, x_unit):
+            inv_rms[(m, x_unit)] = small.tile([P, UNIT_TILES * UNIT_TILES], F32, name="inv_rms")
+            nc.scalar.activation(
+                out=inv_rms[(m, x_unit)][:],
+                in_=sum_sq[(m, x_unit)][:],
+                func=ACT.Abs_reciprocal_sqrt,
+                bias=eps_col[:],
+                scale=1.0 / D,
+            )
+
+        def scale_bank(m, x_unit):
+            acc = accs[(m, x_unit)]
+            inv = inv_rms[(m, x_unit)]
+            if x_unit == 0:
+                stages[m] = stage_pool.tile([P, UNIT_TILES, TOKEN_TILES, D], F32, name="stage")
+            if m >= Q_UNITS + K_UNITS:
+                tiles = slice(x_unit * UNIT_TILES, (x_unit + 1) * UNIT_TILES)
+                nc.vector.tensor_tensor(
+                    out=stages[m][:, :, tiles, :],
+                    in0=acc[:].rearrange("p i (h d) -> p h i d", d=D),
+                    in1=inv[:]
+                    .rearrange("p (i h) -> p h i", h=UNIT_TILES)
+                    .unsqueeze(3)
+                    .to_broadcast([P, UNIT_TILES, UNIT_TILES, D]),
+                    op=ALU.mult,
+                )
+                nc.sync.dma_start(
+                    out=unit_out[m][:, :, x_unit * UNIT_ROWS : (x_unit + 1) * UNIT_ROWS],
+                    in_=stages[m][:, :, tiles, :].rearrange("p h i d -> p h (i d)"),
+                )
+                return
+            if x_unit == 0:
+                terms[m] = terms_pool.tile([P, UNIT_TILES, TOKEN_TILES, 2, D], F32, name="terms")
+            table = rope[0] if m < Q_UNITS else rope[1]
+            for i in range(UNIT_TILES):
+                t = x_unit * UNIT_TILES + i
+                for h in range(UNIT_TILES):
+                    column = i * UNIT_TILES + h
+                    nc.vector.scalar_tensor_tensor(
+                        out=terms[m][:, h, t, :, :],
+                        in0=acc[:, i, h * D : (h + 1) * D].unsqueeze(1).to_broadcast([P, 2, D]),
+                        scalar=inv[:, column : column + 1],
+                        in1=table[:, t, :, :],
+                        op0=ALU.mult,
+                        op1=ALU.mult,
+                    )
+
+        def add_terms(m):
+            pairs = terms[m][:].rearrange("p h t r (c j) -> p (h t r) c j", j=HALF)
+            nc.gpsimd.tensor_tensor(
+                out=stages[m][:].rearrange("p h t (r j) -> p (h t r) j", j=HALF),
+                in0=pairs[:, :, 0, :],
+                in1=pairs[:, :, 1, :],
+                op=ALU.add,
+            )
+
+        def store(m):
+            nc.sync.dma_start(out=unit_out[m], in_=stages[m][:].rearrange("p h t d -> p h (t d)"))
+
+        for s in range(W_UNITS + LAG + 1):
+            m = s - LAG
+            prepare = s < UNITS
+            multiply = 0 <= m < W_UNITS
+            finish = 0 <= m - 1 < W_UNITS
+            if s + LOADS_AHEAD < UNITS:
+                load(s + LOADS_AHEAD)
+            if prepare:
+                transposes(s)
+            if multiply:
+                matmuls(m)
+            if finish:
+                sum_squares(m - 1, 1)
+                inverse_rms(m - 1, 0)
+            if prepare:
+                copy_out(s, 0)
+            if finish:
+                inverse_rms(m - 1, 1)
+            if prepare:
+                for g in range(1, PASSES):
+                    copy_out(s, g)
+            if multiply:
+                sum_squares(m, 0)
+            if finish:
+                scale_bank(m - 1, 0)
+                scale_bank(m - 1, 1)
+                if m - 1 < Q_UNITS + K_UNITS:
+                    add_terms(m - 1)
+            if 0 <= m - 2 < Q_UNITS + K_UNITS:
+                store(m - 2)
+            if prepare:
+                quantise(s, 0)
+                quantise(s, 1)

@@ -20,14 +20,11 @@ HALF = D // 2
 EPS = 1e-6
 PASSES = HID // 512
 PASS_WORDS = 256
-UNIT_ROWS = 256
-UNIT_TILES = UNIT_ROWS // P
-X_UNITS = TOKENS // UNIT_ROWS
+UNIT_HEADS = 2
+UNIT_ROWS = UNIT_HEADS * D
 Q_UNITS, K_UNITS, V_UNITS = 8, 2, 2
 W_UNITS = Q_UNITS + K_UNITS + V_UNITS
-UNITS = X_UNITS + W_UNITS
-LAG = 3
-LOADS_AHEAD = 6
+LOADS_AHEAD = 4
 
 FLOPS = 2 * TOKENS * HID * (W_UNITS * UNIT_ROWS)
 
@@ -49,34 +46,45 @@ def tile_refattention_pa_kernel(
         acc_psum = ctx.enter_context(tc.psum_pool(name="acc", bufs=4))
         ctx.enter_context(tc.manual_schedule())
 
-        gains_row = const.tile([P, 2 * D], BF16, name="gains_row")
-        nc.vector.memset(gains_row[:], 0.0)
-        nc.sync.dma_start(out=gains_row[0:1, 0:D], in_=q_norm_w.rearrange("(o d) -> o d", o=1))
-        nc.sync.dma_start(out=gains_row[0:1, D : 2 * D], in_=k_norm_w.rearrange("(o d) -> o d", o=1))
-        cos_sb = const.tile([P, TOKEN_TILES, D], BF16, name="cos_sb")
-        sin_sb = const.tile([P, TOKEN_TILES, D], BF16, name="sin_sb")
-        nc.sync.dma_start(
-            out=cos_sb[:], in_=cos.flatten_outer_dims().rearrange("(p t) d -> p t d", t=TOKEN_TILES)
-        )
-        nc.sync.dma_start(
-            out=sin_sb[:], in_=sin.flatten_outer_dims().rearrange("(p t) d -> p t d", t=TOKEN_TILES)
-        )
-
         x_rows = hidden_states.flatten_outer_dims().rearrange("(p t) k -> p t k", t=TOKEN_TILES)
-        unit_rows = [x_rows[:, i * UNIT_TILES : (i + 1) * UNIT_TILES, :] for i in range(X_UNITS)]
+        x_raw = []
+        for t in range(TOKEN_TILES):
+            x_raw.append(raw_pool.tile([P, HID], BF16, name="x_raw%d" % t))
+
+        unit_rows = []
         for weight, units in ((Wq, Q_UNITS), (Wk, K_UNITS), (Wv, V_UNITS)):
             for i in range(units):
                 rows = weight[i * UNIT_ROWS : (i + 1) * UNIT_ROWS, :]
                 unit_rows.append(rows.rearrange("(r p) k -> p r k", p=P))
+        w_raw = {}
 
-        raw = {}
+        def load(m, pieces=1):
+            w_raw[m] = raw_pool.tile([P, UNIT_HEADS, HID], BF16, name="w_raw%d" % m)
+            width = HID // pieces
+            for i in range(pieces):
+                k = slice(i * width, (i + 1) * width)
+                nc.sync.dma_start(out=w_raw[m][:, :, k], in_=unit_rows[m][:, :, k])
 
-        def load(unit):
-            raw[unit] = raw_pool.tile([P, UNIT_TILES, HID], BF16, name="raw%d" % unit)
-            nc.sync.dma_start(out=raw[unit][:], in_=unit_rows[unit])
+        gains_row = const.tile([P, 2 * D], BF16, name="gains_row")
+        nc.vector.memset(gains_row[:], 0.0)
+        cos_sb = const.tile([P, TOKEN_TILES, D], BF16, name="cos_sb")
+        sin_sb = const.tile([P, TOKEN_TILES, D], BF16, name="sin_sb")
 
-        for unit in range(LOADS_AHEAD):
-            load(unit)
+        for t in range(TOKEN_TILES):
+            nc.sync.dma_start(out=x_raw[t][:], in_=x_rows[:, t, :])
+            if t == 0:
+                nc.sync.dma_start(out=gains_row[0:1, 0:D], in_=q_norm_w.rearrange("(o d) -> o d", o=1))
+                nc.sync.dma_start(
+                    out=gains_row[0:1, D : 2 * D], in_=k_norm_w.rearrange("(o d) -> o d", o=1)
+                )
+        load(0, pieces=2)
+        for angles, angles_sb in ((cos, cos_sb), (sin, sin_sb)):
+            nc.sync.dma_start(
+                out=angles_sb[:],
+                in_=angles.flatten_outer_dims().rearrange("(p t) d -> p t d", t=TOKEN_TILES),
+            )
+        for m in range(1, LOADS_AHEAD):
+            load(m)
 
         ident = const.tile([P, P], F32, name="ident")
         make_identity(nc, ident[:])
@@ -86,6 +94,167 @@ def tile_refattention_pa_kernel(
         nc.vector.memset(eps_col[:], EPS)
         table_warm = const.tile([P, 1], F32, name="table_warm")
         nc.scalar.activation(out=table_warm[:], in_=eps_col[:], func=ACT.Abs_reciprocal_sqrt)
+
+        unit_out = []
+        for out, units in ((out_0, Q_UNITS), (out_1, K_UNITS), (out_2, V_UNITS)):
+            heads = out.rearrange("o h (p t) d -> p (o h) t d", t=TOKEN_TILES)
+            for i in range(units):
+                unit_out.append(heads[:, i * UNIT_HEADS : (i + 1) * UNIT_HEADS, :, :])
+
+        banks = {}
+        grouped = {}
+        codes = {}
+        scales = {}
+        accs = {}
+        sum_sq = {}
+        inv_rms = {}
+        terms = {}
+        stages = {}
+
+        def transpose_into(bank_columns, words, g, u):
+            every_second = slice(g * PASS_WORDS + u, (g + 1) * PASS_WORDS, 2)
+            nc.tensor.transpose(bank_columns, words[:, every_second], ident[:])
+
+        def copy_bank(engine_copy, grouped_tile, half, bank):
+            half_words = grouped_tile[:].bitcast(F32)[:, half * 512 : (half + 1) * 512]
+            engine_copy(
+                out=half_words.rearrange("p (c u) -> p c u", u=2), in_=bank[:].rearrange("p u c -> p c u")
+            )
+
+        def x_transposes(t):
+            words = x_raw[t][:].bitcast(F32)
+            for pair in range(2):
+                bank = flip_psum.tile([P, 2, 2 * P], F32, tag="flip", name="bank")
+                for i in range(2):
+                    for u in range(2):
+                        transpose_into(bank[:, u, i * P : (i + 1) * P], words, 2 * pair + i, u)
+                banks[("x", t, pair)] = bank
+
+        def x_copy_and_quantise(t):
+            tile = grouped_pool.tile([P, 4 * PASSES * P], BF16, align_bytes=64, name="grouped")
+            copy_bank(nc.scalar.copy, tile, 0, banks[("x", t, 0)])
+            copy_bank(nc.vector.tensor_copy, tile, 1, banks[("x", t, 1)])
+            codes[("x", t)] = const.tile([P, PASSES * P], U32, align_bytes=64, name="x_codes%d" % t)
+            scales[("x", t)] = const.tile([P, PASSES * P], U8, align_bytes=64, name="x_scales%d" % t)
+            nc.vector.quantize_mx(
+                out=codes[("x", t)][:].bitcast(FP8X4), scales=scales[("x", t)][:], in_=tile[:]
+            )
+
+        def transposes(m):
+            words = w_raw[m][:].bitcast(F32)
+            for g in range(PASSES):
+                bank = flip_psum.tile([P, 2, UNIT_ROWS], F32, tag="flip", name="bank")
+                for r in range(UNIT_HEADS):
+                    for u in range(2):
+                        transpose_into(bank[:, u, r * P : (r + 1) * P], words[:, r, :], g, u)
+                banks[(m, g)] = bank
+
+        def copy_out(m, g):
+            pair, i = divmod(g, 2)
+            if i == 0:
+                grouped[(m, pair)] = grouped_pool.tile(
+                    [P, 4 * 2 * UNIT_ROWS], BF16, align_bytes=64, name="grouped"
+                )
+            engine_copy = nc.vector.tensor_copy if (m <= 1 and i == 1) else nc.scalar.copy
+            copy_bank(engine_copy, grouped[(m, pair)], i, banks[(m, g)])
+
+        def quantise(m, pair):
+            if pair == 0:
+                codes[m] = words_pool.tile([P, PASSES * UNIT_ROWS], U32, align_bytes=64, name="codes")
+                scales[m] = words_pool.tile([P, PASSES * UNIT_ROWS], U8, align_bytes=64, name="scales")
+            columns = slice(pair * 2 * UNIT_ROWS, (pair + 1) * 2 * UNIT_ROWS)
+            nc.vector.quantize_mx(
+                out=codes[m][:, columns].bitcast(FP8X4),
+                scales=scales[m][:, columns],
+                in_=grouped[(m, pair)][:],
+            )
+
+        def groups(m):
+            return ((0, 1), (2,), (3,)) if m == W_UNITS - 1 else ((0, 1), (2, 3))
+
+        def matmuls(m):
+            for group in groups(m):
+                acc = acc_psum.tile([P, 2, UNIT_ROWS], F32, tag="acc", name="acc")
+                for i, t in enumerate(group):
+                    accs[(m, t)] = acc[:, i, :]
+                    for g in range(PASSES):
+                        tokens = slice(g * P, (g + 1) * P)
+                        features = slice(g * UNIT_ROWS, (g + 1) * UNIT_ROWS)
+                        nc.tensor.matmul_mx(
+                            out=acc[:, i, :],
+                            lhsT=codes[("x", t)][:, tokens].bitcast(FP8X4),
+                            lhsT_scale=scales[("x", t)][:, tokens],
+                            rhs=codes[m][:, features].bitcast(FP8X4),
+                            rhs_scale=scales[m][:, features],
+                            start=(g == 0),
+                            stop=(g == PASSES - 1),
+                        )
+
+        def sum_squares(m, group):
+            sum_sq[(m, group)] = small.tile([P, len(group) * UNIT_HEADS], F32, name="sum_sq")
+            squares = squares_pool.tile([P, 2, UNIT_ROWS], F32, name="squares")
+            for i, t in enumerate(group):
+                for h in range(UNIT_HEADS):
+                    column = i * UNIT_HEADS + h
+                    nc.scalar.activation(
+                        out=squares[:, i, h * D : (h + 1) * D],
+                        in_=accs[(m, t)][:, h * D : (h + 1) * D],
+                        func=ACT.Square,
+                        accum_out=sum_sq[(m, group)][:, column : column + 1],
+                    )
+
+        def inverse_rms(m, group):
+            inv_rms[(m, group)] = small.tile([P, len(group) * UNIT_HEADS], F32, name="inv_rms")
+            nc.scalar.activation(
+                out=inv_rms[(m, group)][:],
+                in_=sum_sq[(m, group)][:],
+                func=ACT.Abs_reciprocal_sqrt,
+                bias=eps_col[:],
+                scale=1.0 / D,
+            )
+
+        def scale_v(m, group):
+            for i, t in enumerate(group):
+                nc.vector.tensor_tensor(
+                    out=stages[m][:, :, t, :],
+                    in0=accs[(m, t)].rearrange("p (h d) -> p h d", d=D),
+                    in1=inv_rms[(m, group)][:, i * UNIT_HEADS : (i + 1) * UNIT_HEADS]
+                    .unsqueeze(2)
+                    .to_broadcast([P, UNIT_HEADS, D]),
+                    op=ALU.mult,
+                )
+            tiles = slice(group[0], group[-1] + 1)
+            nc.sync.dma_start(out=unit_out[m][:, :, tiles, :], in_=stages[m][:, :, tiles, :])
+
+        def scale_qk(m, group):
+            table = rope[0] if m < Q_UNITS else rope[1]
+            for i, t in enumerate(group):
+                for h in range(UNIT_HEADS):
+                    column = i * UNIT_HEADS + h
+                    nc.vector.scalar_tensor_tensor(
+                        out=terms[m][:, h, t, :, :],
+                        in0=accs[(m, t)][:, h * D : (h + 1) * D].unsqueeze(1).to_broadcast([P, 2, D]),
+                        scalar=inv_rms[(m, group)][:, column : column + 1],
+                        in1=table[:, t, :, :],
+                        op0=ALU.mult,
+                        op1=ALU.mult,
+                    )
+
+        def add_terms(m):
+            pairs = terms[m][:].rearrange("p h t r (c j) -> p (h t r) c j", j=HALF)
+            nc.gpsimd.tensor_tensor(
+                out=stages[m][:].rearrange("p h t (r j) -> p (h t r) j", j=HALF),
+                in0=pairs[:, :, 0, :],
+                in1=pairs[:, :, 1, :],
+                op=ALU.add,
+            )
+
+        def store(m):
+            nc.sync.dma_start(out=unit_out[m], in_=stages[m][:])
+
+        for t in range(TOKEN_TILES):
+            x_transposes(t)
+            x_copy_and_quantise(t)
 
         gains_ps = flip_psum.tile([P, 2 * D], F32, tag="flip", name="gains_ps")
         nc.tensor.matmul(out=gains_ps[:], lhsT=ones[:], rhs=gains_row[:], start=True, stop=True)
@@ -113,183 +282,46 @@ def tile_refattention_pa_kernel(
                 )
             rope.append(table)
 
-        unit_out = []
-        for out, units in ((out_0, Q_UNITS), (out_1, K_UNITS), (out_2, V_UNITS)):
-            heads = out.rearrange("o h (p t) d -> p (o h) (t d)", t=TOKEN_TILES)
-            for i in range(units):
-                unit_out.append(heads[:, i * UNIT_TILES : (i + 1) * UNIT_TILES, :])
-
-        banks = {}
-        grouped = {}
-        codes = {}
-        scales = {}
-        accs = {}
-        sum_sq = {}
-        inv_rms = {}
-        terms = {}
-        stages = {}
-
-        def transposes(unit):
-            words = raw[unit][:].bitcast(F32)
-            for g in range(PASSES):
-                bank = flip_psum.tile([P, 2, UNIT_ROWS], F32, tag="flip", name="bank")
-                for r in range(UNIT_TILES):
-                    for u in range(2):
-                        every_second = slice(g * PASS_WORDS + u, (g + 1) * PASS_WORDS, 2)
-                        nc.tensor.transpose(
-                            bank[:, u, r * P : (r + 1) * P], words[:, r, every_second], ident[:]
-                        )
-                banks[(unit, g)] = bank
-
-        def copy_out(unit, g):
-            pair, i = divmod(g, 2)
-            if i == 0:
-                grouped[(unit, pair)] = grouped_pool.tile(
-                    [P, 2 * 4 * UNIT_ROWS], BF16, align_bytes=64, name="grouped"
-                )
-            grouped_words = grouped[(unit, pair)][:].bitcast(F32)
-            engine_copy = nc.vector.tensor_copy if (unit <= LAG and i == 1) else nc.scalar.copy
-            engine_copy(
-                out=grouped_words[:, i * 2 * UNIT_ROWS : (i + 1) * 2 * UNIT_ROWS].rearrange(
-                    "p (c u) -> p c u", u=2
-                ),
-                in_=banks[(unit, g)][:].rearrange("p u c -> p c u"),
-            )
-
-        def quantise(unit, pair):
-            if pair == 0:
-                pool = const if unit < X_UNITS else words_pool
-                codes[unit] = pool.tile(
-                    [P, PASSES * UNIT_ROWS], U32, align_bytes=64, name="codes%d" % min(unit, X_UNITS)
-                )
-                scales[unit] = pool.tile(
-                    [P, PASSES * UNIT_ROWS], U8, align_bytes=64, name="scales%d" % min(unit, X_UNITS)
-                )
-            columns = slice(pair * 2 * UNIT_ROWS, (pair + 1) * 2 * UNIT_ROWS)
-            nc.vector.quantize_mx(
-                out=codes[unit][:, columns].bitcast(FP8X4),
-                scales=scales[unit][:, columns],
-                in_=grouped[(unit, pair)][:],
-            )
-
-        def matmuls(m):
-            w = m + X_UNITS
-            for x_unit in range(X_UNITS):
-                acc = acc_psum.tile([P, UNIT_TILES, UNIT_ROWS], F32, tag="acc", name="acc")
-                for i in range(UNIT_TILES):
-                    for g in range(PASSES):
-                        tokens = slice(g * UNIT_ROWS + i * P, g * UNIT_ROWS + (i + 1) * P)
-                        features = slice(g * UNIT_ROWS, (g + 1) * UNIT_ROWS)
-                        nc.tensor.matmul_mx(
-                            out=acc[:, i, :],
-                            lhsT=codes[x_unit][:, tokens].bitcast(FP8X4),
-                            lhsT_scale=scales[x_unit][:, tokens],
-                            rhs=codes[w][:, features].bitcast(FP8X4),
-                            rhs_scale=scales[w][:, features],
-                            start=(g == 0),
-                            stop=(g == PASSES - 1),
-                        )
-                accs[(m, x_unit)] = acc
-
-        def sum_squares(m, x_unit):
-            acc = accs[(m, x_unit)]
-            sum_sq[(m, x_unit)] = small.tile([P, UNIT_TILES * UNIT_TILES], F32, name="sum_sq")
-            squares = squares_pool.tile([P, UNIT_TILES, UNIT_ROWS], F32, name="squares")
-            for i in range(UNIT_TILES):
-                for h in range(UNIT_TILES):
-                    column = i * UNIT_TILES + h
-                    nc.scalar.activation(
-                        out=squares[:, i, h * D : (h + 1) * D],
-                        in_=acc[:, i, h * D : (h + 1) * D],
-                        func=ACT.Square,
-                        accum_out=sum_sq[(m, x_unit)][:, column : column + 1],
-                    )
-
-        def inverse_rms(m, x_unit):
-            inv_rms[(m, x_unit)] = small.tile([P, UNIT_TILES * UNIT_TILES], F32, name="inv_rms")
-            nc.scalar.activation(
-                out=inv_rms[(m, x_unit)][:],
-                in_=sum_sq[(m, x_unit)][:],
-                func=ACT.Abs_reciprocal_sqrt,
-                bias=eps_col[:],
-                scale=1.0 / D,
-            )
-
-        def scale_bank(m, x_unit):
-            acc = accs[(m, x_unit)]
-            inv = inv_rms[(m, x_unit)]
-            if x_unit == 0:
-                stages[m] = stage_pool.tile([P, UNIT_TILES, TOKEN_TILES, D], F32, name="stage")
-            if m >= Q_UNITS + K_UNITS:
-                tiles = slice(x_unit * UNIT_TILES, (x_unit + 1) * UNIT_TILES)
-                nc.vector.tensor_tensor(
-                    out=stages[m][:, :, tiles, :],
-                    in0=acc[:].rearrange("p i (h d) -> p h i d", d=D),
-                    in1=inv[:]
-                    .rearrange("p (i h) -> p h i", h=UNIT_TILES)
-                    .unsqueeze(3)
-                    .to_broadcast([P, UNIT_TILES, UNIT_TILES, D]),
-                    op=ALU.mult,
-                )
-                nc.sync.dma_start(
-                    out=unit_out[m][:, :, x_unit * UNIT_ROWS : (x_unit + 1) * UNIT_ROWS],
-                    in_=stages[m][:, :, tiles, :].rearrange("p h i d -> p h (i d)"),
-                )
-                return
-            if x_unit == 0:
-                terms[m] = terms_pool.tile([P, UNIT_TILES, TOKEN_TILES, 2, D], F32, name="terms")
-            table = rope[0] if m < Q_UNITS else rope[1]
-            for i in range(UNIT_TILES):
-                t = x_unit * UNIT_TILES + i
-                for h in range(UNIT_TILES):
-                    column = i * UNIT_TILES + h
-                    nc.vector.scalar_tensor_tensor(
-                        out=terms[m][:, h, t, :, :],
-                        in0=acc[:, i, h * D : (h + 1) * D].unsqueeze(1).to_broadcast([P, 2, D]),
-                        scalar=inv[:, column : column + 1],
-                        in1=table[:, t, :, :],
-                        op0=ALU.mult,
-                        op1=ALU.mult,
-                    )
-
-        def add_terms(m):
-            pairs = terms[m][:].rearrange("p h t r (c j) -> p (h t r) c j", j=HALF)
-            nc.gpsimd.tensor_tensor(
-                out=stages[m][:].rearrange("p h t (r j) -> p (h t r) j", j=HALF),
-                in0=pairs[:, :, 0, :],
-                in1=pairs[:, :, 1, :],
-                op=ALU.add,
-            )
-
-        def store(m):
-            nc.sync.dma_start(out=unit_out[m], in_=stages[m][:].rearrange("p h t d -> p h (t d)"))
-
-        for s in range(W_UNITS + LAG + 1):
-            m = s - LAG
-            prepare = s < UNITS
+        for s in range(W_UNITS + 2):
+            m = s - 1
+            prepare = s < W_UNITS
             multiply = 0 <= m < W_UNITS
-            finish = 0 <= m - 1 < W_UNITS
-            if s + LOADS_AHEAD < UNITS:
+            finish = 0 <= m - 1
+            if s + LOADS_AHEAD < W_UNITS:
                 load(s + LOADS_AHEAD)
             if prepare:
                 transposes(s)
             if multiply:
                 matmuls(m)
             if finish:
-                sum_squares(m - 1, 1)
-                inverse_rms(m - 1, 0)
+                first_group, later_groups = groups(m - 1)[0], groups(m - 1)[1:]
+                for group in later_groups:
+                    sum_squares(m - 1, group)
+                    if not prepare:
+                        inverse_rms(m - 1, group)
+                if prepare or multiply:
+                    inverse_rms(m - 1, first_group)
             if prepare:
                 copy_out(s, 0)
-            if finish:
-                inverse_rms(m - 1, 1)
+            if finish and prepare:
+                for group in later_groups:
+                    inverse_rms(m - 1, group)
             if prepare:
                 for g in range(1, PASSES):
                     copy_out(s, g)
             if multiply:
-                sum_squares(m, 0)
+                sum_squares(m, groups(m)[0])
+                if m == W_UNITS - 1:
+                    inverse_rms(m, groups(m)[0])
             if finish:
-                scale_bank(m - 1, 0)
-                scale_bank(m - 1, 1)
+                stages[m - 1] = stage_pool.tile([P, UNIT_HEADS, TOKEN_TILES, D], F32, name="stage")
+                if m - 1 < Q_UNITS + K_UNITS:
+                    terms[m - 1] = terms_pool.tile([P, UNIT_HEADS, TOKEN_TILES, 2, D], F32, name="terms")
+                for group in groups(m - 1):
+                    if m - 1 < Q_UNITS + K_UNITS:
+                        scale_qk(m - 1, group)
+                    else:
+                        scale_v(m - 1, group)
                 if m - 1 < Q_UNITS + K_UNITS:
                     add_terms(m - 1)
             if 0 <= m - 2 < Q_UNITS + K_UNITS:

@@ -95,6 +95,8 @@ def tile_refattention_pa_kernel(
         table_warm = const.tile([P, 1], F32, name="table_warm")
         nc.scalar.activation(out=table_warm[:], in_=eps_col[:], func=ACT.Abs_reciprocal_sqrt)
 
+        pace = const.tile([P, 1], F32, name="pace")
+
         unit_out = []
         for out, units in ((out_0, Q_UNITS), (out_1, K_UNITS), (out_2, V_UNITS)):
             heads = out.rearrange("o h (p t) d -> p (o h) t d", t=TOKEN_TILES)
@@ -241,6 +243,7 @@ def tile_refattention_pa_kernel(
                     )
 
         def add_terms(m):
+            stages[m] = stage_pool.tile([P, UNIT_HEADS, TOKEN_TILES, D], F32, name="stage")
             pairs = terms[m][:].rearrange("p h t r (c j) -> p (h t r) c j", j=HALF)
             nc.gpsimd.tensor_tensor(
                 out=stages[m][:].rearrange("p h t (r j) -> p (h t r) j", j=HALF),
@@ -314,18 +317,21 @@ def tile_refattention_pa_kernel(
                 if m == W_UNITS - 1:
                     inverse_rms(m, groups(m)[0])
             if finish:
-                stages[m - 1] = stage_pool.tile([P, UNIT_HEADS, TOKEN_TILES, D], F32, name="stage")
                 if m - 1 < Q_UNITS + K_UNITS:
                     terms[m - 1] = terms_pool.tile([P, UNIT_HEADS, TOKEN_TILES, 2, D], F32, name="terms")
-                for group in groups(m - 1):
-                    if m - 1 < Q_UNITS + K_UNITS:
+                    for group in groups(m - 1):
                         scale_qk(m - 1, group)
-                    else:
+                    newest = terms[m - 1][:, 0, 0, 0, 0:1]
+                else:
+                    stages[m - 1] = stage_pool.tile([P, UNIT_HEADS, TOKEN_TILES, D], F32, name="stage")
+                    for group in groups(m - 1):
                         scale_v(m - 1, group)
-                if m - 1 < Q_UNITS + K_UNITS:
-                    add_terms(m - 1)
-            if 0 <= m - 2 < Q_UNITS + K_UNITS:
-                store(m - 2)
+                    newest = stages[m - 1][:, 0, 0, 0:1]
+                if 0 <= m - 2 < Q_UNITS + K_UNITS:
+                    nc.gpsimd.tensor_copy(out=pace[:], in_=newest)
+                    add_terms(m - 2)
+            if 0 <= m - 3 < Q_UNITS + K_UNITS:
+                store(m - 3)
             if prepare:
                 quantise(s, 0)
                 quantise(s, 1)

@@ -26,6 +26,8 @@ Q_UNITS, K_UNITS, V_UNITS = 8, 2, 2
 W_UNITS = Q_UNITS + K_UNITS + V_UNITS
 LOADS_AHEAD = 4
 
+PACED_UNITS = Q_UNITS
+
 FLOPS = 2 * TOKENS * HID * (W_UNITS * UNIT_ROWS)
 
 
@@ -41,7 +43,7 @@ def tile_refattention_pa_kernel(
         small = ctx.enter_context(tc.tile_pool(name="small", bufs=6))
         squares_pool = ctx.enter_context(tc.tile_pool(name="squares", bufs=3))
         terms_pool = ctx.enter_context(tc.tile_pool(name="terms", bufs=2))
-        stage_pool = ctx.enter_context(tc.tile_pool(name="stage", bufs=3))
+        stage_pool = ctx.enter_context(tc.tile_pool(name="stage", bufs=4))
         flip_psum = ctx.enter_context(tc.psum_pool(name="flip", bufs=4))
         acc_psum = ctx.enter_context(tc.psum_pool(name="acc", bufs=4))
         ctx.enter_context(tc.manual_schedule())
@@ -176,7 +178,10 @@ def tile_refattention_pa_kernel(
 
         def matmuls(m):
             for group in groups(m):
-                acc = acc_psum.tile([P, 2, UNIT_ROWS], F32, tag="acc", name="acc")
+                if len(group) == 2:
+                    acc = acc_psum.tile([P, 2, UNIT_ROWS], F32, tag="acc", name="acc")
+                else:
+                    acc = flip_psum.tile([P, 2, UNIT_ROWS], F32, tag="flip", name="bank")
                 for i, t in enumerate(group):
                     accs[(m, t)] = acc[:, i, :]
                     for g in range(PASSES):
@@ -327,11 +332,15 @@ def tile_refattention_pa_kernel(
                     for group in groups(m - 1):
                         scale_v(m - 1, group)
                     newest = stages[m - 1][:, 0, 0, 0:1]
-                if 0 <= m - 2 < Q_UNITS + K_UNITS:
+                if 0 <= m - 2 < PACED_UNITS:
                     nc.gpsimd.tensor_copy(out=pace[:], in_=newest)
                     add_terms(m - 2)
-            if 0 <= m - 3 < Q_UNITS + K_UNITS:
+                if PACED_UNITS <= m - 1 < Q_UNITS + K_UNITS:
+                    add_terms(m - 1)
+            if 0 <= m - 3 < PACED_UNITS:
                 store(m - 3)
+            if PACED_UNITS <= m - 2 < Q_UNITS + K_UNITS:
+                store(m - 2)
             if prepare:
                 quantise(s, 0)
                 quantise(s, 1)

@@ -28,6 +28,8 @@ LOADS_AHEAD = 4
 
 PACED_UNITS = Q_UNITS
 
+SORT_AHEAD = 2
+
 FLOPS = 2 * TOKENS * HID * (W_UNITS * UNIT_ROWS)
 
 
@@ -44,6 +46,7 @@ def tile_refattention_pa_kernel(
         squares_pool = ctx.enter_context(tc.tile_pool(name="squares", bufs=3))
         terms_pool = ctx.enter_context(tc.tile_pool(name="terms", bufs=2))
         stage_pool = ctx.enter_context(tc.tile_pool(name="stage", bufs=4))
+        sorted_pool = ctx.enter_context(tc.tile_pool(name="sorted", bufs=2))
         flip_psum = ctx.enter_context(tc.psum_pool(name="flip", bufs=4))
         acc_psum = ctx.enter_context(tc.psum_pool(name="acc", bufs=4))
         ctx.enter_context(tc.manual_schedule())
@@ -106,6 +109,7 @@ def tile_refattention_pa_kernel(
                 unit_out.append(heads[:, i * UNIT_HEADS : (i + 1) * UNIT_HEADS, :, :])
 
         banks = {}
+        sorted_words = {}
         grouped = {}
         codes = {}
         scales = {}
@@ -144,13 +148,30 @@ def tile_refattention_pa_kernel(
                 out=codes[("x", t)][:].bitcast(FP8X4), scales=scales[("x", t)][:], in_=tile[:]
             )
 
+        def sort_words(engine_copy, name, m, passes):
+            tile = sorted_pool.tile([P, 2, UNIT_HEADS, len(passes) * P], F32, name=name)
+            words = w_raw[m][:].bitcast(F32)[:, :, passes[0] * PASS_WORDS : (passes[-1] + 1) * PASS_WORDS]
+            engine_copy(out=tile[:], in_=words.rearrange("p r (n u) -> p u r n", u=2))
+            for i, g in enumerate(passes):
+                sorted_words[(m, g)] = tile[:, :, :, i * P : (i + 1) * P]
+
+        def vector_passes(m):
+            return range(PASSES) if SORT_AHEAD <= m < 2 * SORT_AHEAD else []
+
+        def scalar_passes(m):
+            return [PASSES - 1] if 2 * SORT_AHEAD <= m < W_UNITS else []
+
         def transposes(m):
             words = w_raw[m][:].bitcast(F32)
             for g in range(PASSES):
                 bank = flip_psum.tile([P, 2, UNIT_ROWS], F32, tag="flip", name="bank")
                 for r in range(UNIT_HEADS):
                     for u in range(2):
-                        transpose_into(bank[:, u, r * P : (r + 1) * P], words[:, r, :], g, u)
+                        bank_columns = bank[:, u, r * P : (r + 1) * P]
+                        if (m, g) in sorted_words:
+                            nc.tensor.transpose(bank_columns, sorted_words[(m, g)][:, u, r, :], ident[:])
+                        else:
+                            transpose_into(bank_columns, words[:, r, :], g, u)
                 banks[(m, g)] = bank
 
         def copy_out(m, g):
@@ -317,6 +338,8 @@ def tile_refattention_pa_kernel(
             if prepare:
                 for g in range(1, PASSES):
                     copy_out(s, g)
+            if scalar_passes(s + SORT_AHEAD):
+                sort_words(nc.scalar.copy, "s_sorted", s + SORT_AHEAD, scalar_passes(s + SORT_AHEAD))
             if multiply:
                 sum_squares(m, groups(m)[0])
                 if m == W_UNITS - 1:
@@ -344,3 +367,5 @@ def tile_refattention_pa_kernel(
             if prepare:
                 quantise(s, 0)
                 quantise(s, 1)
+            if vector_passes(s + SORT_AHEAD):
+                sort_words(nc.vector.tensor_copy, "v_sorted%d" % len(vector_passes(s + SORT_AHEAD)), s + SORT_AHEAD, vector_passes(s + SORT_AHEAD))

@@ -29,6 +29,7 @@ LOADS_AHEAD = 4
 PACED_UNITS = Q_UNITS
 
 SORT_AHEAD = 2
+K_TABLE_STEP = 3
 
 FLOPS = 2 * TOKENS * HID * (W_UNITS * UNIT_ROWS)
 
@@ -76,19 +77,22 @@ def tile_refattention_pa_kernel(
         sin_sb = const.tile([P, TOKEN_TILES, D], BF16, name="sin_sb")
 
         for t in range(TOKEN_TILES):
-            nc.sync.dma_start(out=x_raw[t][:], in_=x_rows[:, t, :])
+            width = HID // 2 if t == 0 else HID
+            for k0 in range(0, HID, width):
+                nc.sync.dma_start(out=x_raw[t][:, k0 : k0 + width], in_=x_rows[:, t, k0 : k0 + width])
             if t == 0:
                 nc.sync.dma_start(out=gains_row[0:1, 0:D], in_=q_norm_w.rearrange("(o d) -> o d", o=1))
                 nc.sync.dma_start(
                     out=gains_row[0:1, D : 2 * D], in_=k_norm_w.rearrange("(o d) -> o d", o=1)
                 )
         load(0, pieces=2)
+        load(1)
         for angles, angles_sb in ((cos, cos_sb), (sin, sin_sb)):
             nc.sync.dma_start(
                 out=angles_sb[:],
                 in_=angles.flatten_outer_dims().rearrange("(p t) d -> p t d", t=TOKEN_TILES),
             )
-        for m in range(1, LOADS_AHEAD):
+        for m in range(2, LOADS_AHEAD):
             load(m)
 
         ident = const.tile([P, P], F32, name="ident")
@@ -141,7 +145,7 @@ def tile_refattention_pa_kernel(
         def x_copy_and_quantise(t):
             tile = grouped_pool.tile([P, 4 * PASSES * P], BF16, align_bytes=64, name="grouped")
             copy_bank(nc.scalar.copy, tile, 0, banks[("x", t, 0)])
-            copy_bank(nc.vector.tensor_copy, tile, 1, banks[("x", t, 1)])
+            copy_bank(nc.vector.tensor_copy if t % 2 == 0 else nc.scalar.copy, tile, 1, banks[("x", t, 1)])
             codes[("x", t)] = const.tile([P, PASSES * P], U32, align_bytes=64, name="x_codes%d" % t)
             scales[("x", t)] = const.tile([P, PASSES * P], U8, align_bytes=64, name="x_scales%d" % t)
             nc.vector.quantize_mx(
@@ -156,7 +160,7 @@ def tile_refattention_pa_kernel(
                 sorted_words[(m, g)] = tile[:, :, :, i * P : (i + 1) * P]
 
         def vector_passes(m):
-            return range(PASSES) if SORT_AHEAD <= m < 2 * SORT_AHEAD else []
+            return [0] if 2 * SORT_AHEAD <= m < W_UNITS else []
 
         def scalar_passes(m):
             return [PASSES - 1] if 2 * SORT_AHEAD <= m < W_UNITS else []
@@ -180,7 +184,7 @@ def tile_refattention_pa_kernel(
                 grouped[(m, pair)] = grouped_pool.tile(
                     [P, 4 * 2 * UNIT_ROWS], BF16, align_bytes=64, name="grouped"
                 )
-            engine_copy = nc.vector.tensor_copy if (m <= 1 and i == 1) else nc.scalar.copy
+            engine_copy = nc.vector.tensor_copy if (m == 0 and i == 1) else nc.scalar.copy
             copy_bank(engine_copy, grouped[(m, pair)], i, banks[(m, g)])
 
         def quantise(m, pair):
@@ -292,24 +296,23 @@ def tile_refattention_pa_kernel(
         nc.scalar.copy(out=gains[:], in_=gains_ps[:])
         nc.scalar.mul(out=minus_gains[:], in_=gains_ps[:], mul=-1.0)
 
-        rope = []
-        for which in range(2):
+        rope = [const.tile([P, TOKEN_TILES, 2, D], F32, name="rope%d" % which) for which in range(2)]
+
+        def rope_quarter(which, quarter):
             w_lo = slice(which * D, which * D + HALF)
             w_hi = slice(which * D + HALF, (which + 1) * D)
-            table = const.tile([P, TOKEN_TILES, 2, D], F32, name="rope%d" % which)
-            for row, columns, angles, gain in (
+            row, columns, angles, gain = (
                 (0, slice(0, HALF), cos_sb[:, :, 0:HALF], gains[:, w_lo]),
                 (0, slice(HALF, D), sin_sb[:, :, 0:HALF], minus_gains[:, w_hi]),
                 (1, slice(0, HALF), sin_sb[:, :, HALF:D], gains[:, w_lo]),
                 (1, slice(HALF, D), cos_sb[:, :, HALF:D], gains[:, w_hi]),
-            ):
-                nc.gpsimd.tensor_tensor(
-                    out=table[:, :, row, columns],
-                    in0=angles,
-                    in1=gain.unsqueeze(1).to_broadcast([P, TOKEN_TILES, HALF]),
-                    op=ALU.mult,
-                )
-            rope.append(table)
+            )[quarter]
+            nc.vector.tensor_tensor(
+                out=rope[which][:, :, row, columns],
+                in0=angles,
+                in1=gain.unsqueeze(1).to_broadcast([P, TOKEN_TILES, HALF]),
+                op=ALU.mult,
+            )
 
         for s in range(W_UNITS + 2):
             m = s - 1
@@ -344,19 +347,19 @@ def tile_refattention_pa_kernel(
                 sum_squares(m, groups(m)[0])
                 if m == W_UNITS - 1:
                     inverse_rms(m, groups(m)[0])
+            if s + 1 in (2, 3):
+                sort_words(nc.vector.tensor_copy, "v_sorted", s + 1, range(PASSES))
             if finish:
                 if m - 1 < Q_UNITS + K_UNITS:
                     terms[m - 1] = terms_pool.tile([P, UNIT_HEADS, TOKEN_TILES, 2, D], F32, name="terms")
                     for group in groups(m - 1):
                         scale_qk(m - 1, group)
-                    newest = terms[m - 1][:, 0, 0, 0, 0:1]
                 else:
                     stages[m - 1] = stage_pool.tile([P, UNIT_HEADS, TOKEN_TILES, D], F32, name="stage")
                     for group in groups(m - 1):
                         scale_v(m - 1, group)
-                    newest = stages[m - 1][:, 0, 0, 0:1]
                 if 0 <= m - 2 < PACED_UNITS:
-                    nc.gpsimd.tensor_copy(out=pace[:], in_=newest)
+                    nc.gpsimd.tensor_copy(out=pace[:], in_=inv_rms[(m - 1, groups(m - 1)[0])][:, 0:1])
                     add_terms(m - 2)
                 if PACED_UNITS <= m - 1 < Q_UNITS + K_UNITS:
                     add_terms(m - 1)
@@ -368,4 +371,9 @@ def tile_refattention_pa_kernel(
                 quantise(s, 0)
                 quantise(s, 1)
             if vector_passes(s + SORT_AHEAD):
-                sort_words(nc.vector.tensor_copy, "v_sorted%d" % len(vector_passes(s + SORT_AHEAD)), s + SORT_AHEAD, vector_passes(s + SORT_AHEAD))
+                sort_words(nc.vector.tensor_copy, "v_part", s + SORT_AHEAD, vector_passes(s + SORT_AHEAD))
+            if s == 0:
+                for quarter in range(4):
+                    rope_quarter(0, quarter)
+            if K_TABLE_STEP <= s < K_TABLE_STEP + 4:
+                rope_quarter(1, s - K_TABLE_STEP)

@@ -26,7 +26,7 @@ Q_UNITS, K_UNITS, V_UNITS = 8, 2, 2
 W_UNITS = Q_UNITS + K_UNITS + V_UNITS
 LOADS_AHEAD = 4
 
-PACED_UNITS = Q_UNITS
+LAST_ROTATED = Q_UNITS + K_UNITS - 1
 
 SORT_AHEAD = 2
 K_TABLE_STEP = 3
@@ -86,14 +86,14 @@ def tile_refattention_pa_kernel(
                     out=gains_row[0:1, D : 2 * D], in_=k_norm_w.rearrange("(o d) -> o d", o=1)
                 )
         load(0, pieces=2)
-        load(1)
+        load(1, pieces=2)
         for angles, angles_sb in ((cos, cos_sb), (sin, sin_sb)):
             nc.sync.dma_start(
                 out=angles_sb[:],
                 in_=angles.flatten_outer_dims().rearrange("(p t) d -> p t d", t=TOKEN_TILES),
             )
         for m in range(2, LOADS_AHEAD):
-            load(m)
+            load(m, pieces=2)
 
         ident = const.tile([P, P], F32, name="ident")
         make_identity(nc, ident[:])
@@ -145,7 +145,7 @@ def tile_refattention_pa_kernel(
         def x_copy_and_quantise(t):
             tile = grouped_pool.tile([P, 4 * PASSES * P], BF16, align_bytes=64, name="grouped")
             copy_bank(nc.scalar.copy, tile, 0, banks[("x", t, 0)])
-            copy_bank(nc.vector.tensor_copy if t % 2 == 0 else nc.scalar.copy, tile, 1, banks[("x", t, 1)])
+            copy_bank(nc.vector.tensor_copy if t == 0 else nc.scalar.copy, tile, 1, banks[("x", t, 1)])
             codes[("x", t)] = const.tile([P, PASSES * P], U32, align_bytes=64, name="x_codes%d" % t)
             scales[("x", t)] = const.tile([P, PASSES * P], U8, align_bytes=64, name="x_scales%d" % t)
             nc.vector.quantize_mx(
@@ -272,13 +272,12 @@ def tile_refattention_pa_kernel(
                         op1=ALU.mult,
                     )
 
-        def add_terms(m):
-            stages[m] = stage_pool.tile([P, UNIT_HEADS, TOKEN_TILES, D], F32, name="stage")
-            pairs = terms[m][:].rearrange("p h t r (c j) -> p (h t r) c j", j=HALF)
-            nc.gpsimd.tensor_tensor(
-                out=stages[m][:].rearrange("p h t (r j) -> p (h t r) j", j=HALF),
-                in0=pairs[:, :, 0, :],
-                in1=pairs[:, :, 1, :],
+        def add_terms(engine, m, tiles):
+            pairs = terms[m][:, :, tiles, :, :].rearrange("p h t r (c j) -> p h (t r) c j", j=HALF)
+            engine.tensor_tensor(
+                out=stages[m][:, :, tiles, :].rearrange("p h t (r j) -> p h (t r) j", j=HALF),
+                in0=pairs[:, :, :, 0, :],
+                in1=pairs[:, :, :, 1, :],
                 op=ALU.add,
             )
 
@@ -348,9 +347,11 @@ def tile_refattention_pa_kernel(
                 if m == W_UNITS - 1:
                     inverse_rms(m, groups(m)[0])
             if s + 1 in (2, 3):
-                sort_words(nc.vector.tensor_copy, "v_sorted", s + 1, range(PASSES))
+                for half in (range(0, PASSES // 2), range(PASSES // 2, PASSES)):
+                    sort_words(nc.vector.tensor_copy, "v_sorted%d" % half[0], s + 1, half)
             if finish:
                 if m - 1 < Q_UNITS + K_UNITS:
+                    stages[m - 1] = stage_pool.tile([P, UNIT_HEADS, TOKEN_TILES, D], F32, name="stage")
                     terms[m - 1] = terms_pool.tile([P, UNIT_HEADS, TOKEN_TILES, 2, D], F32, name="terms")
                     for group in groups(m - 1):
                         scale_qk(m - 1, group)
@@ -358,18 +359,18 @@ def tile_refattention_pa_kernel(
                     stages[m - 1] = stage_pool.tile([P, UNIT_HEADS, TOKEN_TILES, D], F32, name="stage")
                     for group in groups(m - 1):
                         scale_v(m - 1, group)
-                if 0 <= m - 2 < PACED_UNITS:
+                if 0 <= m - 2 < LAST_ROTATED:
                     nc.gpsimd.tensor_copy(out=pace[:], in_=inv_rms[(m - 1, groups(m - 1)[0])][:, 0:1])
-                    add_terms(m - 2)
-                if PACED_UNITS <= m - 1 < Q_UNITS + K_UNITS:
-                    add_terms(m - 1)
-            if 0 <= m - 3 < PACED_UNITS:
+                    add_terms(nc.gpsimd, m - 2, slice(0, TOKEN_TILES))
+            if 0 <= m - 3 < LAST_ROTATED - 1:
                 store(m - 3)
-            if PACED_UNITS <= m - 2 < Q_UNITS + K_UNITS:
-                store(m - 2)
             if prepare:
                 quantise(s, 0)
                 quantise(s, 1)
+            if m - 1 == LAST_ROTATED:
+                add_terms(nc.vector, m - 1, slice(0, TOKEN_TILES))
+                store(m - 2)
+                store(m - 1)
             if vector_passes(s + SORT_AHEAD):
                 sort_words(nc.vector.tensor_copy, "v_part", s + SORT_AHEAD, vector_passes(s + SORT_AHEAD))
             if s == 0:

from contextlib import ExitStack

import concourse.mybir as mybir
from concourse.masks import make_identity

F32 = mybir.dt.float32
BF16 = mybir.dt.bfloat16
U32 = mybir.dt.uint32
U8 = mybir.dt.uint8
FP8X4 = mybir.dt.float8_e4m3fn_x4
ACT = mybir.ActivationFunctionType
ALU = mybir.AluOpType

P = 128
TOKENS = 512
TOKEN_TILES = TOKENS // P
HID = 2048
D = 128
HALF = D // 2
EPS = 1e-6
PASSES = HID // 512
PASS_WORDS = 256
UNIT_HEADS = 2
UNIT_ROWS = UNIT_HEADS * D
Q_UNITS, K_UNITS, V_UNITS = 8, 2, 2
W_UNITS = Q_UNITS + K_UNITS + V_UNITS
LOADS_AHEAD = 4

LAST_ROTATED = Q_UNITS + K_UNITS - 1

SORT_AHEAD = 2
K_TABLE_STEP = 3

FLOPS = 2 * TOKENS * HID * (W_UNITS * UNIT_ROWS)


def tile_refattention_pa_kernel(
    tc, hidden_states, cos, sin, Wq, Wk, Wv, q_norm_w, k_norm_w, out_0, out_1, out_2
):
    nc = tc.nc
    with ExitStack() as ctx:
        const = ctx.enter_context(tc.tile_pool(name="const", bufs=1))
        raw_pool = ctx.enter_context(tc.tile_pool(name="raw", bufs=1))
        grouped_pool = ctx.enter_context(tc.tile_pool(name="grouped", bufs=4))
        words_pool = ctx.enter_context(tc.tile_pool(name="words", bufs=4))
        small = ctx.enter_context(tc.tile_pool(name="small", bufs=6))
        squares_pool = ctx.enter_context(tc.tile_pool(name="squares", bufs=3))
        terms_pool = ctx.enter_context(tc.tile_pool(name="terms", bufs=2))
        stage_pool = ctx.enter_context(tc.tile_pool(name="stage", bufs=4))
        sorted_pool = ctx.enter_context(tc.tile_pool(name="sorted", bufs=2))
        flip_psum = ctx.enter_context(tc.psum_pool(name="flip", bufs=4))
        acc_psum = ctx.enter_context(tc.psum_pool(name="acc", bufs=4))
        ctx.enter_context(tc.manual_schedule())

        x_rows = hidden_states.flatten_outer_dims().rearrange("(p t) k -> p t k", t=TOKEN_TILES)
        x_raw = []
        for t in range(TOKEN_TILES):
            x_raw.append(raw_pool.tile([P, HID], BF16, name="x_raw%d" % t))

        unit_rows = []
        for weight, units in ((Wq, Q_UNITS), (Wk, K_UNITS), (Wv, V_UNITS)):
            for i in range(units):
                rows = weight[i * UNIT_ROWS : (i + 1) * UNIT_ROWS, :]
                unit_rows.append(rows.rearrange("(r p) k -> p r k", p=P))
        w_raw = {}

        def load(m, pieces=1):
            w_raw[m] = raw_pool.tile([P, UNIT_HEADS, HID], BF16, name="w_raw%d" % m)
            width = HID // pieces
            for i in range(pieces):
                k = slice(i * width, (i + 1) * width)
                nc.sync.dma_start(out=w_raw[m][:, :, k], in_=unit_rows[m][:, :, k])

        gains_row = const.tile([P, 2 * D], BF16, name="gains_row")
        nc.vector.memset(gains_row[:], 0.0)
        cos_sb = const.tile([P, TOKEN_TILES, D], BF16, name="cos_sb")
        sin_sb = const.tile([P, TOKEN_TILES, D], BF16, name="sin_sb")

        for t in range(TOKEN_TILES):
            width = HID // 2 if t == 0 else HID
            for k0 in range(0, HID, width):
                nc.sync.dma_start(out=x_raw[t][:, k0 : k0 + width], in_=x_rows[:, t, k0 : k0 + width])
            if t == 0:
                nc.sync.dma_start(out=gains_row[0:1, 0:D], in_=q_norm_w.rearrange("(o d) -> o d", o=1))
                nc.sync.dma_start(
                    out=gains_row[0:1, D : 2 * D], in_=k_norm_w.rearrange("(o d) -> o d", o=1)
                )
        load(0, pieces=2)
        load(1, pieces=2)
        for angles, angles_sb in ((cos, cos_sb), (sin, sin_sb)):
            nc.sync.dma_start(
                out=angles_sb[:],
                in_=angles.flatten_outer_dims().rearrange("(p t) d -> p t d", t=TOKEN_TILES),
            )
        for m in range(2, LOADS_AHEAD):
            load(m, pieces=2)

        ident = const.tile([P, P], F32, name="ident")
        make_identity(nc, ident[:])
        ones = const.tile([P, P], BF16, name="ones")
        nc.vector.memset(ones[:], 1.0)
        eps_col = const.tile([P, 1], F32, name="eps_col")
        nc.vector.memset(eps_col[:], EPS)
        table_warm = const.tile([P, 1], F32, name="table_warm")
        nc.scalar.activation(out=table_warm[:], in_=eps_col[:], func=ACT.Abs_reciprocal_sqrt)

        pace = const.tile([P, 1], F32, name="pace")

        unit_out = []
        for out, units in ((out_0, Q_UNITS), (out_1, K_UNITS), (out_2, V_UNITS)):
            heads = out.rearrange("o h (p t) d -> p (o h) t d", t=TOKEN_TILES)
            for i in range(units):
                unit_out.append(heads[:, i * UNIT_HEADS : (i + 1) * UNIT_HEADS, :, :])

        banks = {}
        sorted_words = {}
        grouped = {}
        codes = {}
        scales = {}
        accs = {}
        sum_sq = {}
        inv_rms = {}
        terms = {}
        stages = {}

        def transpose_into(bank_columns, words, g, u):
            every_second = slice(g * PASS_WORDS + u, (g + 1) * PASS_WORDS, 2)
            nc.tensor.transpose(bank_columns, words[:, every_second], ident[:])

        def copy_bank(engine_copy, grouped_tile, half, bank):
            half_words = grouped_tile[:].bitcast(F32)[:, half * 512 : (half + 1) * 512]
            engine_copy(
                out=half_words.rearrange("p (c u) -> p c u", u=2), in_=bank[:].rearrange("p u c -> p c u")
            )

        def x_transposes(t):
            words = x_raw[t][:].bitcast(F32)
            for pair in range(2):
                bank = flip_psum.tile([P, 2, 2 * P], F32, tag="flip", name="bank")
                for i in range(2):
                    for u in range(2):
                        transpose_into(bank[:, u, i * P : (i + 1) * P], words, 2 * pair + i, u)
                banks[("x", t, pair)] = bank

        def x_copy_and_quantise(t):
            tile = grouped_pool.tile([P, 4 * PASSES * P], BF16, align_bytes=64, name="grouped")
            copy_bank(nc.scalar.copy, tile, 0, banks[("x", t, 0)])
            copy_bank(nc.vector.tensor_copy if t == 0 else nc.scalar.copy, tile, 1, banks[("x", t, 1)])
            codes[("x", t)] = const.tile([P, PASSES * P], U32, align_bytes=64, name="x_codes%d" % t)
            scales[("x", t)] = const.tile([P, PASSES * P], U8, align_bytes=64, name="x_scales%d" % t)
            nc.vector.quantize_mx(
                out=codes[("x", t)][:].bitcast(FP8X4), scales=scales[("x", t)][:], in_=tile[:]
            )

        def sort_words(engine_copy, name, m, passes):
            tile = sorted_pool.tile([P, 2, UNIT_HEADS, len(passes) * P], F32, name=name)
            words = w_raw[m][:].bitcast(F32)[:, :, passes[0] * PASS_WORDS : (passes[-1] + 1) * PASS_WORDS]
            engine_copy(out=tile[:], in_=words.rearrange("p r (n u) -> p u r n", u=2))
            for i, g in enumerate(passes):
                sorted_words[(m, g)] = tile[:, :, :, i * P : (i + 1) * P]

        def vector_passes(m):
            return [0] if 2 * SORT_AHEAD <= m < W_UNITS else []

        def scalar_passes(m):
            return [PASSES - 1] if 2 * SORT_AHEAD <= m < W_UNITS else []

        def transposes(m):
            words = w_raw[m][:].bitcast(F32)
            for g in range(PASSES):
                bank = flip_psum.tile([P, 2, UNIT_ROWS], F32, tag="flip", name="bank")
                for r in range(UNIT_HEADS):
                    for u in range(2):
                        bank_columns = bank[:, u, r * P : (r + 1) * P]
                        if (m, g) in sorted_words:
                            nc.tensor.transpose(bank_columns, sorted_words[(m, g)][:, u, r, :], ident[:])
                        else:
                            transpose_into(bank_columns, words[:, r, :], g, u)
                banks[(m, g)] = bank

        def copy_out(m, g):
            pair, i = divmod(g, 2)
            if i == 0:
                grouped[(m, pair)] = grouped_pool.tile(
                    [P, 4 * 2 * UNIT_ROWS], BF16, align_bytes=64, name="grouped"
                )
            engine_copy = nc.vector.tensor_copy if (m == 0 and i == 1) else nc.scalar.copy
            copy_bank(engine_copy, grouped[(m, pair)], i, banks[(m, g)])

        def quantise(m, pair):
            if pair == 0:
                codes[m] = words_pool.tile([P, PASSES * UNIT_ROWS], U32, align_bytes=64, name="codes")
                scales[m] = words_pool.tile([P, PASSES * UNIT_ROWS], U8, align_bytes=64, name="scales")
            columns = slice(pair * 2 * UNIT_ROWS, (pair + 1) * 2 * UNIT_ROWS)
            nc.vector.quantize_mx(
                out=codes[m][:, columns].bitcast(FP8X4),
                scales=scales[m][:, columns],
                in_=grouped[(m, pair)][:],
            )

        def groups(m):
            return ((0, 1), (2,), (3,)) if m == W_UNITS - 1 else ((0, 1), (2, 3))

        def matmuls(m):
            for group in groups(m):
                if len(group) == 2:
                    acc = acc_psum.tile([P, 2, UNIT_ROWS], F32, tag="acc", name="acc")
                else:
                    acc = flip_psum.tile([P, 2, UNIT_ROWS], F32, tag="flip", name="bank")
                for i, t in enumerate(group):
                    accs[(m, t)] = acc[:, i, :]
                    for g in range(PASSES):
                        tokens = slice(g * P, (g + 1) * P)
                        features = slice(g * UNIT_ROWS, (g + 1) * UNIT_ROWS)
                        nc.tensor.matmul_mx(
                            out=acc[:, i, :],
                            lhsT=codes[("x", t)][:, tokens].bitcast(FP8X4),
                            lhsT_scale=scales[("x", t)][:, tokens],
                            rhs=codes[m][:, features].bitcast(FP8X4),
                            rhs_scale=scales[m][:, features],
                            start=(g == 0),
                            stop=(g == PASSES - 1),
                        )

        def sum_squares(m, group):
            sum_sq[(m, group)] = small.tile([P, len(group) * UNIT_HEADS], F32, name="sum_sq")
            squares = squares_pool.tile([P, 2, UNIT_ROWS], F32, name="squares")
            for i, t in enumerate(group):
                for h in range(UNIT_HEADS):
                    column = i * UNIT_HEADS + h
                    nc.scalar.activation(
                        out=squares[:, i, h * D : (h + 1) * D],
                        in_=accs[(m, t)][:, h * D : (h + 1) * D],
                        func=ACT.Square,
                        accum_out=sum_sq[(m, group)][:, column : column + 1],
                    )

        def inverse_rms(m, group):
            inv_rms[(m, group)] = small.tile([P, len(group) * UNIT_HEADS], F32, name="inv_rms")
            nc.scalar.activation(
                out=inv_rms[(m, group)][:],
                in_=sum_sq[(m, group)][:],
                func=ACT.Abs_reciprocal_sqrt,
                bias=eps_col[:],
                scale=1.0 / D,
            )

        def scale_v(m, group):
            for i, t in enumerate(group):
                nc.vector.tensor_tensor(
                    out=stages[m][:, :, t, :],
                    in0=accs[(m, t)].rearrange("p (h d) -> p h d", d=D),
                    in1=inv_rms[(m, group)][:, i * UNIT_HEADS : (i + 1) * UNIT_HEADS]
                    .unsqueeze(2)
                    .to_broadcast([P, UNIT_HEADS, D]),
                    op=ALU.mult,
                )
            tiles = slice(group[0], group[-1] + 1)
            nc.sync.dma_start(out=unit_out[m][:, :, tiles, :], in_=stages[m][:, :, tiles, :])

        def scale_qk(m, group):
            table = rope[0] if m < Q_UNITS else rope[1]
            for i, t in enumerate(group):
                for h in range(UNIT_HEADS):
                    column = i * UNIT_HEADS + h
                    nc.vector.scalar_tensor_tensor(
                        out=terms[m][:, h, t, :, :],
                        in0=accs[(m, t)][:, h * D : (h + 1) * D].unsqueeze(1).to_broadcast([P, 2, D]),
                        scalar=inv_rms[(m, group)][:, column : column + 1],
                        in1=table[:, t, :, :],
                        op0=ALU.mult,
                        op1=ALU.mult,
                    )

        def add_terms(engine, m, tiles):
            pairs = terms[m][:, :, tiles, :, :].rearrange("p h t r (c j) -> p h (t r) c j", j=HALF)
            engine.tensor_tensor(
                out=stages[m][:, :, tiles, :].rearrange("p h t (r j) -> p h (t r) j", j=HALF),
                in0=pairs[:, :, :, 0, :],
                in1=pairs[:, :, :, 1, :],
                op=ALU.add,
            )

        def store(m):
            nc.sync.dma_start(out=unit_out[m], in_=stages[m][:])

        for t in range(TOKEN_TILES):
            x_transposes(t)
            x_copy_and_quantise(t)

        gains_ps = flip_psum.tile([P, 2 * D], F32, tag="flip", name="gains_ps")
        nc.tensor.matmul(out=gains_ps[:], lhsT=ones[:], rhs=gains_row[:], start=True, stop=True)
        gains = const.tile([P, 2 * D], F32, name="gains")
        minus_gains = const.tile([P, 2 * D], F32, name="minus_gains")
        nc.scalar.copy(out=gains[:], in_=gains_ps[:])
        nc.scalar.mul(out=minus_gains[:], in_=gains_ps[:], mul=-1.0)

        rope = [const.tile([P, TOKEN_TILES, 2, D], F32, name="rope%d" % which) for which in range(2)]

        def rope_quarter(which, quarter):
            w_lo = slice(which * D, which * D + HALF)
            w_hi = slice(which * D + HALF, (which + 1) * D)
            row, columns, angles, gain = (
                (0, slice(0, HALF), cos_sb[:, :, 0:HALF], gains[:, w_lo]),
                (0, slice(HALF, D), sin_sb[:, :, 0:HALF], minus_gains[:, w_hi]),
                (1, slice(0, HALF), sin_sb[:, :, HALF:D], gains[:, w_lo]),
                (1, slice(HALF, D), cos_sb[:, :, HALF:D], gains[:, w_hi]),
            )[quarter]
            nc.vector.tensor_tensor(
                out=rope[which][:, :, row, columns],
                in0=angles,
                in1=gain.unsqueeze(1).to_broadcast([P, TOKEN_TILES, HALF]),
                op=ALU.mult,
            )

        for s in range(W_UNITS + 2):
            m = s - 1
            prepare = s < W_UNITS
            multiply = 0 <= m < W_UNITS
            finish = 0 <= m - 1
            if s + LOADS_AHEAD < W_UNITS:
                load(s + LOADS_AHEAD)
            if prepare:
                transposes(s)
            if multiply:
                matmuls(m)
            if finish:
                first_group, later_groups = groups(m - 1)[0], groups(m - 1)[1:]
                for group in later_groups:
                    sum_squares(m - 1, group)
                    if not prepare:
                        inverse_rms(m - 1, group)
                if prepare or multiply:
                    inverse_rms(m - 1, first_group)
            if prepare:
                copy_out(s, 0)
            if finish and prepare:
                for group in later_groups:
                    inverse_rms(m - 1, group)
            if prepare:
                for g in range(1, PASSES):
                    copy_out(s, g)
            if scalar_passes(s + SORT_AHEAD):
                sort_words(nc.scalar.copy, "s_sorted", s + SORT_AHEAD, scalar_passes(s + SORT_AHEAD))
            if multiply:
                sum_squares(m, groups(m)[0])
                if m == W_UNITS - 1:
                    inverse_rms(m, groups(m)[0])
            if s + 1 in (2, 3):
                for half in (range(0, PASSES // 2), range(PASSES // 2, PASSES)):
                    sort_words(nc.vector.tensor_copy, "v_sorted%d" % half[0], s + 1, half)
            if finish:
                if m - 1 < Q_UNITS + K_UNITS:
                    stages[m - 1] = stage_pool.tile([P, UNIT_HEADS, TOKEN_TILES, D], F32, name="stage")
                    terms[m - 1] = terms_pool.tile([P, UNIT_HEADS, TOKEN_TILES, 2, D], F32, name="terms")
                    for group in groups(m - 1):
                        scale_qk(m - 1, group)
                else:
                    stages[m - 1] = stage_pool.tile([P, UNIT_HEADS, TOKEN_TILES, D], F32, name="stage")
                    for group in groups(m - 1):
                        scale_v(m - 1, group)
                if 0 <= m - 2 < LAST_ROTATED:
                    nc.gpsimd.tensor_copy(out=pace[:], in_=inv_rms[(m - 1, groups(m - 1)[0])][:, 0:1])
                    add_terms(nc.gpsimd, m - 2, slice(0, TOKEN_TILES))
            if 0 <= m - 3 < LAST_ROTATED - 1:
                store(m - 3)
            if prepare:
                quantise(s, 0)
                quantise(s, 1)
            if m - 1 == LAST_ROTATED:
                add_terms(nc.vector, m - 1, slice(0, TOKEN_TILES))
                store(m - 2)
                store(m - 1)
            if vector_passes(s + SORT_AHEAD):
                sort_words(nc.vector.tensor_copy, "v_part", s + SORT_AHEAD, vector_passes(s + SORT_AHEAD))
            if s == 0:
                for quarter in range(4):
                    rope_quarter(0, quarter)
            if K_TABLE_STEP <= s < K_TABLE_STEP + 4:
                rope_quarter(1, s - K_TABLE_STEP)
